import numpy as np
import ml_dtypes


def mxq(x, axis, fmt="e4m3"):
    dtype, down = {"e4m3": (ml_dtypes.float8_e4m3fn, 7), "e5m2": (ml_dtypes.float8_e5m2, 14)}[fmt]
    v = np.moveaxis(np.asarray(x, np.float32).astype(ml_dtypes.bfloat16).astype(np.float64), axis, -1)
    blocks = v.reshape(v.shape[:-1] + (-1, 32))
    amax = np.abs(blocks).max(-1, keepdims=True)
    byte = np.maximum(np.where(amax > 0, np.frexp(amax)[1] - 1 + 127, 0) - down, 1)
    scale = np.exp2(byte - 127.0)
    codes = (blocks / scale).astype(np.float32).astype(dtype).astype(np.float64)
    return np.moveaxis((codes * scale).reshape(v.shape), -1, axis)


WIDE = False


def mx_kscale(k):
    if not WIDE:
        return np.ones(k)
    levels = np.array([10, -10, 5, -5, 0])
    a = np.random.permutation(np.resize(levels, k // 512 * 4)).reshape(k // 512, 4)
    idx = np.arange(k)
    return np.exp2(a[idx // 512, idx % 128 // 32])


BF16 = ml_dtypes.bfloat16


def bf(x):
    return np.asarray(x, np.float32).astype(BF16)


def f64(x):
    return np.asarray(x).astype(np.float64)


B, S, D, E, NS, C = 1, 1024, 512, 512, 256, 512


def softmax(z):
    e = np.exp(z - z.max(-1, keepdims=True))
    return e / e.sum(-1, keepdims=True)


def setup_inputs():
    s, t = mx_kscale(D), mx_kscale(E)
    return {"x": bf(np.random.standard_normal((B, S, D)) * s),
            "Wk": bf(np.random.standard_normal((D, E)) / np.sqrt(D) / s[:, None] * t),
            "bk": bf(np.random.standard_normal(E) * 0.2 * t),
            "Wq": bf(np.random.standard_normal((D, E)) / np.sqrt(D) / s[:, None] * t),
            "bq": bf(np.random.standard_normal(E) * 0.2 * t),
            "slot_keys": bf(np.random.standard_normal((NS, E)) / t),
            "scale": bf((2.0 + 0.2 * np.random.standard_normal(1)) / np.sqrt(E))}


def reference(x, Wk, bk, Wq, bq, slot_keys, scale):
    xq = mxq(f64(x), 2, "e4m3")
    sq = mxq(f64(slot_keys), 1, "e4m3")
    k = (xq @ mxq(f64(Wk), 0, "e4m3")) + f64(bk)
    q = (xq @ mxq(f64(Wq), 0, "e4m3")) + f64(bq)
    ww = softmax((mxq(k, 2, "e4m3") @ sq.T) * f64(scale))
    rw = softmax((mxq(q, 2, "e4m3") @ sq.T) * f64(scale))
    return ww, rw

@@ -1,0 +1,300 @@
+from contextlib import ExitStack
+
+import concourse.mybir as mybir
+from concourse.masks import make_identity
+
+F32 = mybir.dt.float32
+BF16 = mybir.dt.bfloat16
+U32 = mybir.dt.uint32
+U8 = mybir.dt.uint8
+FP8X4 = mybir.dt.float8_e4m3fn_x4
+ACT = mybir.ActivationFunctionType
+ALU = mybir.AluOpType
+AXIS = mybir.AxisListType
+
+P = 128
+PACK = 4
+TOKENS = 1024
+D = P * PACK
+E = P * PACK
+SLOTS = 256
+PROJECTIONS = 2
+PAIR = 2
+N_PAIRS = TOKENS // (PAIR * P)
+E_TILES = E // P
+SLOT_TILES = SLOTS // P
+ALIGN = 64
+
+FLOPS = PROJECTIONS * 2 * TOKENS * (D * E + E * SLOTS)
+
+
+def tile_slotmemoryphasor_pa_kernel(tc, x, Wk, bk, Wq, bq, slot_keys, scale, out_0, out_1):
+    nc = tc.nc
+    weights = (Wk, Wq)
+    x_pairs = x.flatten_outer_dims().rearrange("(c p i) d -> c p (i d)", p=P, i=PAIR)
+    out_pairs = (
+        out_0.flatten_outer_dims().rearrange("(c p i) n -> c p (i n)", p=P, i=PAIR),
+        out_1.flatten_outer_dims().rearrange("(c p i) n -> c p (i n)", p=P, i=PAIR),
+    )
+    units = [(w, c) for w in range(PROJECTIONS) for c in range(N_PAIRS)]
+    n_units = len(units)
+
+    with ExitStack() as ctx:
+        keep = ctx.enter_context(tc.tile_pool(name="keep", bufs=1))
+        work = ctx.enter_context(tc.tile_pool(name="work", bufs=3))
+        psum_t = ctx.enter_context(tc.psum_pool(name="psum_t", bufs=2))
+        psum_k = ctx.enter_context(tc.psum_pool(name="psum_k", bufs=2 * PAIR))
+        psum_s = ctx.enter_context(tc.psum_pool(name="psum_s", bufs=2))
+
+        x_raw = [keep.tile([P, PAIR * D], BF16, name="x_raw%d" % c) for c in range(N_PAIRS)]
+        w_raw = [keep.tile([P, PACK, E], BF16, name="w_raw%d" % w) for w in range(PROJECTIONS)]
+        slot_raw = keep.tile([P, SLOT_TILES, E], BF16)
+        scale_raw = keep.tile([P, 1], BF16)
+        bias_rows = keep.tile([P, P], BF16)
+
+        def load_x(c):
+            nc.sync.dma_start(out=x_raw[c][:], in_=x_pairs[c])
+
+        def load_w(w):
+            nc.sync.dma_start(
+                out=w_raw[w][:].rearrange("p (h r) e -> p h (r e)", h=2),
+                in_=weights[w].rearrange("(h p r) e -> p h (r e)", h=2, r=2),
+            )
+
+        load_w(0)
+        load_x(0)
+        nc.sync.dma_start(out=slot_raw[:], in_=slot_keys.rearrange("(j p) e -> p j e", p=P))
+        for c in range(1, N_PAIRS):
+            load_x(c)
+        load_w(1)
+        nc.scalar.dma_start(out=scale_raw[:], in_=scale.partition_broadcast(P))
+        nc.vector.memset(bias_rows[:], 0.0)
+        nc.scalar.dma_start(out=bias_rows[0:E_TILES, :], in_=bk.rearrange("(m p) -> m p", p=P))
+        nc.scalar.dma_start(out=bias_rows[E_TILES : 2 * E_TILES, :], in_=bq.rearrange("(m p) -> m p", p=P))
+
+        ident_f32 = keep.tile([P, P], F32)
+        make_identity(nc, ident_f32[:])
+        ident_bf16 = keep.tile([P, P], BF16)
+        make_identity(nc, ident_bf16[:])
+
+        scale_sign = keep.tile([P, 1], F32)
+        nc.scalar.activation(out=scale_sign[:], in_=scale_raw[:], func=ACT.Sign)
+        scale_abs = keep.tile([P, 1], F32)
+        nc.scalar.activation(out=scale_abs[:], in_=scale_raw[:], func=ACT.Abs)
+        scale_neg_abs = keep.tile([P, 1], F32)
+        nc.scalar.mul(out=scale_neg_abs[:], in_=scale_abs[:], mul=-1.0)
+
+        bias = keep.tile([P, PROJECTIONS * E_TILES], F32)
+
+        def prepare_bias():
+            bias_t = psum_t.tile([P, P], BF16, tag="t")
+            nc.tensor.transpose(bias_t[:], bias_rows[:], ident_bf16[:])
+            nc.vector.tensor_copy(out=bias[:], in_=bias_t[:, 0 : PROJECTIONS * E_TILES])
+
+        x_grouped = [
+            keep.tile([P, PAIR * P * PACK], BF16, name="x_grouped%d" % c, align_bytes=ALIGN) for c in range(N_PAIRS)
+        ]
+        x_codes = keep.tile([P, TOKENS], U32, align_bytes=ALIGN)
+        x_scales = keep.tile([P, TOKENS], U8, align_bytes=ALIGN)
+
+        def transpose_x(c):
+            words = x_raw[c][:].bitcast(F32)
+            x_t = psum_t.tile([P, PAIR, 2, P], F32, tag="t")
+            for i in range(PAIR):
+                for h in range(2):
+                    first = (2 * i + h) * P
+                    nc.tensor.transpose(x_t[:, i, h, :], words[:, first : first + P], ident_f32[:])
+            nc.scalar.copy(
+                out=x_grouped[c][:].bitcast(F32).rearrange("p (i s h) -> p i s h", i=PAIR, h=2),
+                in_=x_t[:].rearrange("p i h s -> p i s h"),
+            )
+
+        def quantise_x(c):
+            cols = slice(c * PAIR * P, (c + 1) * PAIR * P)
+            nc.vector.quantize_mx(out=x_codes[:, cols].bitcast(FP8X4), scales=x_scales[:, cols], in_=x_grouped[c][:])
+
+        w_grouped = [
+            keep.tile([P, E, PACK], BF16, name="w_grouped%d" % w, align_bytes=ALIGN) for w in range(PROJECTIONS)
+        ]
+        w_codes = [keep.tile([P, E], U32, name="w_codes%d" % w, align_bytes=ALIGN) for w in range(PROJECTIONS)]
+        w_scales = [keep.tile([P, E], U8, name="w_scales%d" % w, align_bytes=ALIGN) for w in range(PROJECTIONS)]
+
+        def regroup_w(w, copy):
+            copy(
+                out=w_grouped[w][:].rearrange("p (c i) t -> p c t i", i=4),
+                in_=w_raw[w][:].rearrange("p t (c i) -> p c t i", i=4),
+            )
+
+        def quantise_w(w):
+            nc.vector.quantize_mx(
+                out=w_codes[w][:].bitcast(FP8X4),
+                scales=w_scales[w][:],
+                in_=w_grouped[w][:].rearrange("p e t -> p (e t)"),
+            )
+
+        slot_grouped = keep.tile([P, SLOTS, PACK], BF16, align_bytes=ALIGN)
+        slot_codes = keep.tile([P, SLOTS], U32, align_bytes=ALIGN)
+        slot_scales = keep.tile([P, SLOTS], U8, align_bytes=ALIGN)
+
+        def transpose_slots():
+            slot_t = psum_t.tile([P, PACK, SLOTS], BF16, tag="t")
+            for j in range(SLOT_TILES):
+                for t in range(PACK):
+                    nc.tensor.transpose(
+                        slot_t[:, t, j * P : (j + 1) * P], slot_raw[:, j, t * P : (t + 1) * P], ident_bf16[:]
+                    )
+            nc.scalar.activation(
+                out=slot_grouped[:],
+                in_=slot_t[:].rearrange("p t n -> p n t"),
+                func=ACT.Copy,
+                scale=scale_sign[:, 0:1],
+            )
+
+        def quantise_slots():
+            nc.vector.quantize_mx(
+                out=slot_codes[:].bitcast(FP8X4),
+                scales=slot_scales[:],
+                in_=slot_grouped[:].rearrange("p n t -> p (n t)"),
+            )
+
+        kt_banks = {}
+        k_grouped = {}
+        k_operand = {}
+        score_bank = {}
+        shifts = {}
+        exps = {}
+
+        def quantise_operands_of(u):
+            w, c = units[u]
+            if c == 0:
+                quantise_w(w)
+            if w == 0:
+                quantise_x(c)
+
+        def project(u):
+            w, c = units[u]
+            kt_banks[u] = []
+            for i in range(PAIR):
+                tokens = slice((c * PAIR + i) * P, (c * PAIR + i + 1) * P)
+                kt = psum_k.tile([P, E_TILES, P], F32)
+                for m in range(E_TILES):
+                    e_cols = slice(m * P, (m + 1) * P)
+                    nc.tensor.matmul_mx(
+                        out=kt[:, m, :],
+                        lhsT=w_codes[w][:, e_cols].bitcast(FP8X4),
+                        lhsT_scale=w_scales[w][:, e_cols],
+                        rhs=x_codes[:, tokens].bitcast(FP8X4),
+                        rhs_scale=x_scales[:, tokens],
+                        start=True,
+                        stop=True,
+                    )
+                kt_banks[u].append(kt)
+
+        def add_bias(u):
+            w, c = units[u]
+            grouped = work.tile([P, PAIR, P, PACK], BF16, align_bytes=ALIGN)
+            for i in range(PAIR):
+                nc.vector.tensor_tensor(
+                    out=grouped[:, i, :, :],
+                    in0=kt_banks[u][i][:].rearrange("p m s -> p s m"),
+                    in1=bias[:, w * E_TILES : (w + 1) * E_TILES].unsqueeze(1).to_broadcast([P, P, PACK]),
+                    op=ALU.add,
+                )
+            k_grouped[u] = grouped
+
+        def quantise_k(u):
+            codes = work.tile([P, PAIR * P], U32, align_bytes=ALIGN)
+            scales = work.tile([P, PAIR * P], U8, align_bytes=ALIGN)
+            nc.vector.quantize_mx(
+                out=codes[:].bitcast(FP8X4),
+                scales=scales[:],
+                in_=k_grouped[u][:].rearrange("p i s m -> p (i s m)"),
+            )
+            k_operand[u] = (codes, scales)
+
+        def score(u):
+            codes, scales = k_operand[u]
+            scores = psum_s.tile([P, PAIR, SLOTS], F32)
+            for i in range(PAIR):
+                tokens = slice(i * P, (i + 1) * P)
+                nc.tensor.matmul_mx(
+                    out=scores[:, i, :],
+                    lhsT=codes[:, tokens].bitcast(FP8X4),
+                    lhsT_scale=scales[:, tokens],
+                    rhs=slot_codes[:].bitcast(FP8X4),
+                    rhs_scale=slot_scales[:],
+                    start=True,
+                    stop=True,
+                )
+            score_bank[u] = scores
+
+        def find_shift(u):
+            top = work.tile([P, PAIR], F32)
+            nc.vector.tensor_reduce(out=top[:], in_=score_bank[u][:], axis=AXIS.X, op=ALU.max)
+            shift = work.tile([P, PAIR], F32)
+            nc.scalar.activation(out=shift[:], in_=top[:], func=ACT.Copy, scale=scale_neg_abs[:, 0:1])
+            shifts[u] = shift
+
+        def exponentials(u):
+            e = work.tile([P, PAIR, SLOTS], F32)
+            total = work.tile([P, PAIR], F32)
+            for i in range(PAIR):
+                nc.scalar.activation(
+                    out=e[:, i, :],
+                    in_=score_bank[u][:, i, :],
+                    func=ACT.Exp,
+                    bias=shifts[u][:, i : i + 1],
+                    scale=scale_abs[:, 0:1],
+                    accum_out=total[:, i : i + 1],
+                )
+            exps[u] = (e, total)
+
+        def normalise_and_store(u):
+            w, c = units[u]
+            e, total = exps[u]
+            inverse = work.tile([P, PAIR], F32)
+            nc.vector.reciprocal(out=inverse[:], in_=total[:])
+            prob = work.tile([P, PAIR, SLOTS], F32)
+            engine = nc.vector if u == n_units - 1 else nc.gpsimd
+            for i in range(PAIR):
+                engine.tensor_scalar(
+                    out=prob[:, i, :],
+                    in0=e[:, i, :],
+                    scalar1=inverse[:, i : i + 1],
+                    scalar2=0.0,
+                    op0=ALU.mult,
+                    op1=ALU.add,
+                )
+            nc.sync.dma_start(out=out_pairs[w][c], in_=prob[:].rearrange("p i n -> p (i n)"))
+
+        with tc.manual_schedule():
+            regroup_w(0, nc.vector.tensor_copy)
+            transpose_x(0)
+            quantise_operands_of(0)
+            transpose_slots()
+            prepare_bias()
+            project(0)
+            for c in range(1, N_PAIRS):
+                transpose_x(c)
+            regroup_w(1, nc.scalar.copy)
+            add_bias(0)
+            quantise_slots()
+            quantise_operands_of(1)
+            for u in range(n_units):
+                if u + 1 < n_units:
+                    project(u + 1)
+                if u + 2 < n_units:
+                    quantise_operands_of(u + 2)
+                if u >= 1:
+                    find_shift(u - 1)
+                    exponentials(u - 1)
+                if u >= 2:
+                    normalise_and_store(u - 2)
+                quantise_k(u)
+                score(u)
+                if u + 1 < n_units:
+                    add_bias(u + 1)
+            find_shift(n_units - 1)
+            exponentials(n_units - 1)
+            normalise_and_store(n_units - 2)
+            normalise_and_store(n_units - 1)

@@ -255,16 +255,11 @@ def tile_slotmemoryphasor_pa_kernel(tc, x, Wk, bk, Wq, bq, slot_keys, scale, out
             inverse = work.tile([P, PAIR], F32)
             nc.vector.reciprocal(out=inverse[:], in_=total[:])
             prob = work.tile([P, PAIR, SLOTS], F32)
-            engine = nc.vector if u == n_units - 1 else nc.gpsimd
             for i in range(PAIR):
-                engine.tensor_scalar(
-                    out=prob[:, i, :],
-                    in0=e[:, i, :],
-                    scalar1=inverse[:, i : i + 1],
-                    scalar2=0.0,
-                    op0=ALU.mult,
-                    op1=ALU.add,
-                )
+                if u == n_units - 1:
+                    nc.vector.tensor_scalar_mul(out=prob[:, i, :], in0=e[:, i, :], scalar1=inverse[:, i : i + 1])
+                else:
+                    nc.scalar.activation(out=prob[:, i, :], in_=e[:, i, :], func=ACT.Copy, scale=inverse[:, i : i + 1])
             nc.sync.dma_start(out=out_pairs[w][c], in_=prob[:].rearrange("p i n -> p (i n)"))
 
         with tc.manual_schedule():

@@ -25,6 +25,8 @@ E_TILES = E // P
 SLOT_TILES = SLOTS // P
 ALIGN = 64
 
+SCALAR_UNITS = (5, 7)
+
 FLOPS = PROJECTIONS * 2 * TOKENS * (D * E + E * SLOTS)
 
 
@@ -41,10 +43,10 @@ def tile_slotmemoryphasor_pa_kernel(tc, x, Wk, bk, Wq, bq, slot_keys, scale, out
 
     with ExitStack() as ctx:
         keep = ctx.enter_context(tc.tile_pool(name="keep", bufs=1))
-        work = ctx.enter_context(tc.tile_pool(name="work", bufs=3))
-        psum_t = ctx.enter_context(tc.psum_pool(name="psum_t", bufs=2))
+        work = ctx.enter_context(tc.tile_pool(name="work", bufs=n_units))
+        psum_t = ctx.enter_context(tc.psum_pool(name="psum_t", bufs=4))
         psum_k = ctx.enter_context(tc.psum_pool(name="psum_k", bufs=2 * PAIR))
-        psum_s = ctx.enter_context(tc.psum_pool(name="psum_s", bufs=2))
+
 
         x_raw = [keep.tile([P, PAIR * D], BF16, name="x_raw%d" % c) for c in range(N_PAIRS)]
         w_raw = [keep.tile([P, PACK, E], BF16, name="w_raw%d" % w) for w in range(PROJECTIONS)]
@@ -55,17 +57,22 @@ def tile_slotmemoryphasor_pa_kernel(tc, x, Wk, bk, Wq, bq, slot_keys, scale, out
         def load_x(c):
             nc.sync.dma_start(out=x_raw[c][:], in_=x_pairs[c])
 
+        def load_x_tile(c, i):
+            nc.sync.dma_start(out=x_raw[c][:, i * D : (i + 1) * D], in_=x_pairs[c][:, i * D : (i + 1) * D])
+
         def load_w(w):
             nc.sync.dma_start(
                 out=w_raw[w][:].rearrange("p (h r) e -> p h (r e)", h=2),
                 in_=weights[w].rearrange("(h p r) e -> p h (r e)", h=2, r=2),
             )
 
+        load_x_tile(0, 0)
         load_w(0)
-        load_x(0)
+        load_x_tile(0, 1)
+        load_x(1)
+        load_x(2)
         nc.sync.dma_start(out=slot_raw[:], in_=slot_keys.rearrange("(j p) e -> p j e", p=P))
-        for c in range(1, N_PAIRS):
-            load_x(c)
+        load_x(3)
         load_w(1)
         nc.scalar.dma_start(out=scale_raw[:], in_=scale.partition_broadcast(P))
         nc.vector.memset(bias_rows[:], 0.0)
@@ -97,21 +104,24 @@ def tile_slotmemoryphasor_pa_kernel(tc, x, Wk, bk, Wq, bq, slot_keys, scale, out
         x_codes = keep.tile([P, TOKENS], U32, align_bytes=ALIGN)
         x_scales = keep.tile([P, TOKENS], U8, align_bytes=ALIGN)
 
-        def transpose_x(c):
+        def transpose_x(c, tiles):
             words = x_raw[c][:].bitcast(F32)
-            x_t = psum_t.tile([P, PAIR, 2, P], F32, tag="t")
-            for i in range(PAIR):
+            n = len(tiles)
+            x_t = psum_t.tile([P, n, 2, P], F32, tag="t")
+            for j, i in enumerate(tiles):
                 for h in range(2):
                     first = (2 * i + h) * P
-                    nc.tensor.transpose(x_t[:, i, h, :], words[:, first : first + P], ident_f32[:])
+                    nc.tensor.transpose(x_t[:, j, h, :], words[:, first : first + P], ident_f32[:])
+            cols = slice(tiles[0] * P * PACK, (tiles[-1] + 1) * P * PACK)
             nc.scalar.copy(
-                out=x_grouped[c][:].bitcast(F32).rearrange("p (i s h) -> p i s h", i=PAIR, h=2),
+                out=x_grouped[c][:, cols].bitcast(F32).rearrange("p (i s h) -> p i s h", i=n, h=2),
                 in_=x_t[:].rearrange("p i h s -> p i s h"),
             )
 
-        def quantise_x(c):
-            cols = slice(c * PAIR * P, (c + 1) * PAIR * P)
-            nc.vector.quantize_mx(out=x_codes[:, cols].bitcast(FP8X4), scales=x_scales[:, cols], in_=x_grouped[c][:])
+        def quantise_x(c, tiles):
+            cols = slice((c * PAIR + tiles[0]) * P, (c * PAIR + tiles[-1] + 1) * P)
+            src = slice(tiles[0] * P * PACK, (tiles[-1] + 1) * P * PACK)
+            nc.vector.quantize_mx(out=x_codes[:, cols].bitcast(FP8X4), scales=x_scales[:, cols], in_=x_grouped[c][:, src])
 
         w_grouped = [
             keep.tile([P, E, PACK], BF16, name="w_grouped%d" % w, align_bytes=ALIGN) for w in range(PROJECTIONS)
@@ -119,17 +129,17 @@ def tile_slotmemoryphasor_pa_kernel(tc, x, Wk, bk, Wq, bq, slot_keys, scale, out
         w_codes = [keep.tile([P, E], U32, name="w_codes%d" % w, align_bytes=ALIGN) for w in range(PROJECTIONS)]
         w_scales = [keep.tile([P, E], U8, name="w_scales%d" % w, align_bytes=ALIGN) for w in range(PROJECTIONS)]
 
-        def regroup_w(w, copy):
+        def regroup_w(w, copy, first, last):
             copy(
-                out=w_grouped[w][:].rearrange("p (c i) t -> p c t i", i=4),
-                in_=w_raw[w][:].rearrange("p t (c i) -> p c t i", i=4),
+                out=w_grouped[w][:, first:last, :].rearrange("p (c i) t -> p c t i", i=4),
+                in_=w_raw[w][:, :, first:last].rearrange("p t (c i) -> p c t i", i=4),
             )
 
-        def quantise_w(w):
+        def quantise_w(w, first, last):
             nc.vector.quantize_mx(
-                out=w_codes[w][:].bitcast(FP8X4),
-                scales=w_scales[w][:],
-                in_=w_grouped[w][:].rearrange("p e t -> p (e t)"),
+                out=w_codes[w][:, first:last].bitcast(FP8X4),
+                scales=w_scales[w][:, first:last],
+                in_=w_grouped[w][:, first:last, :].rearrange("p e t -> p (e t)"),
             )
 
         slot_grouped = keep.tile([P, SLOTS, PACK], BF16, align_bytes=ALIGN)
@@ -158,25 +168,42 @@ def tile_slotmemoryphasor_pa_kernel(tc, x, Wk, bk, Wq, bq, slot_keys, scale, out
             )
 
         kt_banks = {}
+        k_plain = {}
         k_grouped = {}
         k_operand = {}
         score_bank = {}
         shifts = {}
         exps = {}
+        totals = {}
+        inverses = {}
 
-        def quantise_operands_of(u):
-            w, c = units[u]
-            if c == 0:
-                quantise_w(w)
-            if w == 0:
-                quantise_x(c)
+        def by_scalar(u):
+            return u in SCALAR_UNITS
 
         def project(u):
             w, c = units[u]
             kt_banks[u] = []
+            if by_scalar(u):
+                tokens = slice(c * PAIR * P, (c + 1) * PAIR * P)
+                for half in range(2):
+                    kt = psum_k.tile([P, 2, PAIR * P], F32, tag="kt")
+                    for r in range(2):
+                        m = 2 * half + r
+                        e_cols = slice(m * P, (m + 1) * P)
+                        nc.tensor.matmul_mx(
+                            out=kt[:, r, :],
+                            lhsT=w_codes[w][:, e_cols].bitcast(FP8X4),
+                            lhsT_scale=w_scales[w][:, e_cols],
+                            rhs=x_codes[:, tokens].bitcast(FP8X4),
+                            rhs_scale=x_scales[:, tokens],
+                            start=True,
+                            stop=True,
+                        )
+                    kt_banks[u].append(kt)
+                return
             for i in range(PAIR):
                 tokens = slice((c * PAIR + i) * P, (c * PAIR + i + 1) * P)
-                kt = psum_k.tile([P, E_TILES, P], F32)
+                kt = psum_k.tile([P, E_TILES, P], F32, tag="kt")
                 for m in range(E_TILES):
                     e_cols = slice(m * P, (m + 1) * P)
                     nc.tensor.matmul_mx(
@@ -190,35 +217,58 @@ def tile_slotmemoryphasor_pa_kernel(tc, x, Wk, bk, Wq, bq, slot_keys, scale, out
                     )
                 kt_banks[u].append(kt)
 
-        def add_bias(u):
+        def scalar_bias(u):
             w, c = units[u]
-            grouped = work.tile([P, PAIR, P, PACK], BF16, align_bytes=ALIGN)
-            for i in range(PAIR):
+            plain = work.tile([P, E_TILES, PAIR * P], BF16)
+            for m in range(E_TILES):
+                nc.scalar.activation(
+                    out=plain[:, m, :],
+                    in_=kt_banks[u][m // 2][:, m % 2, :],
+                    func=ACT.Identity,
+                    bias=bias[:, w * E_TILES + m : w * E_TILES + m + 1],
+                )
+            k_plain[u] = plain
+
+        def group_k(u, tiles):
+            w, c = units[u]
+            if u not in k_grouped:
+                grouped = work.tile([P, PAIR, P, PACK], BF16, align_bytes=ALIGN)
+                k_grouped[u] = grouped
+            if by_scalar(u):
+                if tiles[0] == 0:
+                    nc.vector.tensor_copy(
+                        out=k_grouped[u][:].rearrange("p i (c j) m -> p (i c) m j", j=4),
+                        in_=k_plain[u][:].rearrange("p m (c j) -> p c m j", j=4),
+                    )
+                return
+            for i in tiles:
                 nc.vector.tensor_tensor(
-                    out=grouped[:, i, :, :],
+                    out=k_grouped[u][:, i, :, :],
                     in0=kt_banks[u][i][:].rearrange("p m s -> p s m"),
                     in1=bias[:, w * E_TILES : (w + 1) * E_TILES].unsqueeze(1).to_broadcast([P, P, PACK]),
                     op=ALU.add,
                 )
-            k_grouped[u] = grouped
 
-        def quantise_k(u):
-            codes = work.tile([P, PAIR * P], U32, align_bytes=ALIGN)
-            scales = work.tile([P, PAIR * P], U8, align_bytes=ALIGN)
-            nc.vector.quantize_mx(
-                out=codes[:].bitcast(FP8X4),
-                scales=scales[:],
-                in_=k_grouped[u][:].rearrange("p i s m -> p (i s m)"),
-            )
-            k_operand[u] = (codes, scales)
-
-        def score(u):
+        def quantise_k(u, tiles):
+            if u not in k_operand:
+                codes = work.tile([P, PAIR * P], U32, align_bytes=ALIGN)
+                scales = work.tile([P, PAIR * P], U8, align_bytes=ALIGN)
+                k_operand[u] = (codes, scales)
             codes, scales = k_operand[u]
-            scores = psum_s.tile([P, PAIR, SLOTS], F32)
-            for i in range(PAIR):
+            cols = slice(tiles[0] * P, (tiles[-1] + 1) * P)
+            nc.vector.quantize_mx(
+                out=codes[:, cols].bitcast(FP8X4),
+                scales=scales[:, cols],
+                in_=k_grouped[u][:, tiles[0] : tiles[-1] + 1, :, :].rearrange("p i s m -> p (i s m)"),
+            )
+
+        def score(u, tiles):
+            codes, scales = k_operand[u]
+            scores = psum_t.tile([P, len(tiles), SLOTS], F32, tag="t")
+            for j, i in enumerate(tiles):
                 tokens = slice(i * P, (i + 1) * P)
                 nc.tensor.matmul_mx(
-                    out=scores[:, i, :],
+                    out=scores[:, j, :],
                     lhsT=codes[:, tokens].bitcast(FP8X4),
                     lhsT_scale=scales[:, tokens],
                     rhs=slot_codes[:].bitcast(FP8X4),
@@ -226,70 +276,127 @@ def tile_slotmemoryphasor_pa_kernel(tc, x, Wk, bk, Wq, bq, slot_keys, scale, out
                     start=True,
                     stop=True,
                 )
+                score_bank[u, i] = scores[:, j, :]
             score_bank[u] = scores
 
-        def find_shift(u):
-            top = work.tile([P, PAIR], F32)
-            nc.vector.tensor_reduce(out=top[:], in_=score_bank[u][:], axis=AXIS.X, op=ALU.max)
-            shift = work.tile([P, PAIR], F32)
-            nc.scalar.activation(out=shift[:], in_=top[:], func=ACT.Copy, scale=scale_neg_abs[:, 0:1])
-            shifts[u] = shift
+        def find_shift(u, tiles):
+            if u not in shifts:
+                top = work.tile([P, PAIR], F32)
+                shift = work.tile([P, PAIR], F32)
+                shifts[u] = (top, shift)
+            top, shift = shifts[u]
+            cols = slice(tiles[0], tiles[-1] + 1)
+            src = score_bank[u][:] if len(tiles) == PAIR else score_bank[u, tiles[0]]
+            nc.vector.tensor_reduce(out=top[:, cols], in_=src, axis=AXIS.X, op=ALU.max)
+            nc.scalar.activation(out=shift[:, cols], in_=top[:, cols], func=ACT.Copy, scale=scale_neg_abs[:, 0:1])
 
-        def exponentials(u):
-            e = work.tile([P, PAIR, SLOTS], F32)
-            total = work.tile([P, PAIR], F32)
-            for i in range(PAIR):
+        def exponentials(u, tiles):
+            if u not in exps:
+                e = work.tile([P, PAIR, SLOTS], F32)
+                exps[u] = e
+                total = work.tile([P, PAIR], F32)
+                totals[u] = total
+            for i in tiles:
                 nc.scalar.activation(
-                    out=e[:, i, :],
-                    in_=score_bank[u][:, i, :],
+                    out=exps[u][:, i, :],
+                    in_=score_bank[u, i],
                     func=ACT.Exp,
-                    bias=shifts[u][:, i : i + 1],
+                    bias=shifts[u][1][:, i : i + 1],
                     scale=scale_abs[:, 0:1],
-                    accum_out=total[:, i : i + 1],
+                    accum_out=totals[u][:, i : i + 1],
                 )
-            exps[u] = (e, total)
 
-        def normalise_and_store(u):
+        def invert_totals(u, tiles):
+            if u not in inverses:
+                inverse = work.tile([P, PAIR], F32)
+                prob = work.tile([P, PAIR, SLOTS], F32)
+                inverses[u] = (inverse, prob)
+            cols = slice(tiles[0], tiles[-1] + 1)
+            nc.vector.reciprocal(out=inverses[u][0][:, cols], in_=totals[u][:, cols])
+
+        def normalise_and_store(u, tiles):
             w, c = units[u]
-            e, total = exps[u]
-            inverse = work.tile([P, PAIR], F32)
-            nc.vector.reciprocal(out=inverse[:], in_=total[:])
-            prob = work.tile([P, PAIR, SLOTS], F32)
-            for i in range(PAIR):
-                if u == n_units - 1:
-                    nc.vector.tensor_scalar_mul(out=prob[:, i, :], in0=e[:, i, :], scalar1=inverse[:, i : i + 1])
+            inverse, prob = inverses[u]
+            for i in tiles:
+                if u >= n_units - 2:
+                    nc.vector.tensor_scalar_mul(out=prob[:, i, :], in0=exps[u][:, i, :], scalar1=inverse[:, i : i + 1])
                 else:
-                    nc.scalar.activation(out=prob[:, i, :], in_=e[:, i, :], func=ACT.Copy, scale=inverse[:, i : i + 1])
-            nc.sync.dma_start(out=out_pairs[w][c], in_=prob[:].rearrange("p i n -> p (i n)"))
+                    nc.gpsimd.tensor_scalar(
+                        out=prob[:, i, :],
+                        in0=exps[u][:, i, :],
+                        scalar1=inverse[:, i : i + 1],
+                        scalar2=0.0,
+                        op0=ALU.mult,
+                        op1=ALU.add,
+                    )
+            cols = slice(tiles[0] * SLOTS, (tiles[-1] + 1) * SLOTS)
+            nc.sync.dma_start(
+                out=out_pairs[w][c][:, cols], in_=prob[:, tiles[0] : tiles[-1] + 1, :].rearrange("p i n -> p (i n)")
+            )
 
+        both = (0, 1)
+        last = n_units - 1
+        half = E // 2
         with tc.manual_schedule():
-            regroup_w(0, nc.vector.tensor_copy)
-            transpose_x(0)
-            quantise_operands_of(0)
-            transpose_slots()
+            transpose_x(0, (0,))
+            regroup_w(0, nc.vector.tensor_copy, 0, half)
+            regroup_w(0, nc.scalar.copy, half + P, E)
+            transpose_x(0, (1,))
+            quantise_x(0, (0,))
+            quantise_w(0, 0, half)
+            regroup_w(0, nc.vector.tensor_copy, half, half + P)
+            quantise_x(0, (1,))
+            transpose_x(1, both)
+            quantise_w(0, half, E)
             prepare_bias()
+            quantise_x(1, both)
             project(0)
-            for c in range(1, N_PAIRS):
-                transpose_x(c)
-            regroup_w(1, nc.scalar.copy)
-            add_bias(0)
+            transpose_x(2, both)
+            project(1)
+            regroup_w(1, nc.scalar.copy, 0, half)
+            transpose_slots()
+            group_k(0, both)
+            quantise_x(2, both)
+            quantise_k(0, both)
+            project(2)
+            transpose_x(3, both)
+            regroup_w(1, nc.scalar.copy, half, E)
+            group_k(1, both)
+            group_k(2, both)
             quantise_slots()
-            quantise_operands_of(1)
-            for u in range(n_units):
-                if u + 1 < n_units:
-                    project(u + 1)
-                if u + 2 < n_units:
-                    quantise_operands_of(u + 2)
-                if u >= 1:
-                    find_shift(u - 1)
-                    exponentials(u - 1)
-                if u >= 2:
-                    normalise_and_store(u - 2)
-                quantise_k(u)
-                score(u)
-                if u + 1 < n_units:
-                    add_bias(u + 1)
-            find_shift(n_units - 1)
-            exponentials(n_units - 1)
-            normalise_and_store(n_units - 2)
-            normalise_and_store(n_units - 1)
+            score(0, both)
+            quantise_k(1, both)
+            score(1, both)
+            quantise_x(3, both)
+            project(3)
+            find_shift(0, both)
+            exponentials(0, both)
+            quantise_w(1, 0, E)
+            for u in range(2, n_units):
+                if u + 2 <= last:
+                    project(u + 2)
+                if u == last:
+                    find_shift(u - 1, both)
+                    exponentials(u - 1, both)
+                    for i in both:
+                        quantise_k(u, (i,))
+                        score(u, (i,))
+                else:
+                    quantise_k(u, both)
+                    score(u, both)
+                if u + 1 <= last:
+                    group_k(u + 1, both)
+                if u + 2 <= last and by_scalar(u + 2):
+                    scalar_bias(u + 2)
+                if u < last:
+                    find_shift(u - 1, both)
+                    exponentials(u - 1, both)
+                invert_totals(u - 2, both)
+                normalise_and_store(u - 2, both)
+            for i in both:
+                find_shift(last, (i,))
+                exponentials(last, (i,))
+            for u in (last - 1, last):
+                for i in both:
+                    invert_totals(u, (i,))
+                    normalise_and_store(u, (i,))

@@ -91,6 +91,14 @@ def tile_slotmemoryphasor_pa_kernel(tc, x, Wk, bk, Wq, bq, slot_keys, scale, out
         scale_neg_abs = keep.tile([P, 1], F32)
         nc.scalar.mul(out=scale_neg_abs[:], in_=scale_abs[:], mul=-1.0)
 
+        zeros = keep.tile([P, 4 * P], BF16)
+        nc.vector.memset(zeros[:], 0.0)
+
+        def warm_up(times):
+            idle = psum_t.tile([P, 4 * P], F32, tag="t")
+            for i in range(times):
+                nc.tensor.matmul(idle[:], zeros[:, 0:P], zeros[:], start=True, stop=True)
+
         bias = keep.tile([P, PROJECTIONS * E_TILES], F32)
 
         def prepare_bias():
@@ -338,15 +346,19 @@ def tile_slotmemoryphasor_pa_kernel(tc, x, Wk, bk, Wq, bq, slot_keys, scale, out
         last = n_units - 1
         half = E // 2
         with tc.manual_schedule():
+            warm_up(4)
             transpose_x(0, (0,))
+            warm_up(1)
             regroup_w(0, nc.vector.tensor_copy, 0, half)
             regroup_w(0, nc.scalar.copy, half + P, E)
             transpose_x(0, (1,))
+            warm_up(1)
             quantise_x(0, (0,))
             quantise_w(0, 0, half)
             regroup_w(0, nc.vector.tensor_copy, half, half + P)
             quantise_x(0, (1,))
             transpose_x(1, both)
+            warm_up(1)
             quantise_w(0, half, E)
             prepare_bias()
             quantise_x(1, both)

@@ -25,7 +25,7 @@ E_TILES = E // P
 SLOT_TILES = SLOTS // P
 ALIGN = 64
 
-SCALAR_UNITS = (5, 7)
+SCALAR_UNITS = (3, 4, 5, 6, 7)
 
 FLOPS = PROJECTIONS * 2 * TOKENS * (D * E + E * SLOTS)
 
@@ -185,30 +185,12 @@ def tile_slotmemoryphasor_pa_kernel(tc, x, Wk, bk, Wq, bq, slot_keys, scale, out
         totals = {}
         inverses = {}
 
-        def by_scalar(u):
-            return u in SCALAR_UNITS
+        def by_scalar(u, i):
+            return i == 1 and u in SCALAR_UNITS
 
         def project(u):
             w, c = units[u]
             kt_banks[u] = []
-            if by_scalar(u):
-                tokens = slice(c * PAIR * P, (c + 1) * PAIR * P)
-                for half in range(2):
-                    kt = psum_k.tile([P, 2, PAIR * P], F32, tag="kt")
-                    for r in range(2):
-                        m = 2 * half + r
-                        e_cols = slice(m * P, (m + 1) * P)
-                        nc.tensor.matmul_mx(
-                            out=kt[:, r, :],
-                            lhsT=w_codes[w][:, e_cols].bitcast(FP8X4),
-                            lhsT_scale=w_scales[w][:, e_cols],
-                            rhs=x_codes[:, tokens].bitcast(FP8X4),
-                            rhs_scale=x_scales[:, tokens],
-                            start=True,
-                            stop=True,
-                        )
-                    kt_banks[u].append(kt)
-                return
             for i in range(PAIR):
                 tokens = slice((c * PAIR + i) * P, (c * PAIR + i + 1) * P)
                 kt = psum_k.tile([P, E_TILES, P], F32, tag="kt")
@@ -225,37 +207,36 @@ def tile_slotmemoryphasor_pa_kernel(tc, x, Wk, bk, Wq, bq, slot_keys, scale, out
                     )
                 kt_banks[u].append(kt)
 
-        def scalar_bias(u):
+        def scalar_bias(u, i):
             w, c = units[u]
-            plain = work.tile([P, E_TILES, PAIR * P], BF16)
+            plain = work.tile([P, E_TILES, P], BF16)
             for m in range(E_TILES):
                 nc.scalar.activation(
                     out=plain[:, m, :],
-                    in_=kt_banks[u][m // 2][:, m % 2, :],
+                    in_=kt_banks[u][i][:, m, :],
                     func=ACT.Identity,
                     bias=bias[:, w * E_TILES + m : w * E_TILES + m + 1],
                 )
-            k_plain[u] = plain
+            k_plain[u, i] = plain
 
         def group_k(u, tiles):
             w, c = units[u]
             if u not in k_grouped:
                 grouped = work.tile([P, PAIR, P, PACK], BF16, align_bytes=ALIGN)
                 k_grouped[u] = grouped
-            if by_scalar(u):
-                if tiles[0] == 0:
-                    nc.vector.tensor_copy(
-                        out=k_grouped[u][:].rearrange("p i (c j) m -> p (i c) m j", j=4),
-                        in_=k_plain[u][:].rearrange("p m (c j) -> p c m j", j=4),
-                    )
-                return
             for i in tiles:
-                nc.vector.tensor_tensor(
-                    out=k_grouped[u][:, i, :, :],
-                    in0=kt_banks[u][i][:].rearrange("p m s -> p s m"),
-                    in1=bias[:, w * E_TILES : (w + 1) * E_TILES].unsqueeze(1).to_broadcast([P, P, PACK]),
-                    op=ALU.add,
-                )
+                if by_scalar(u, i):
+                    nc.vector.tensor_copy(
+                        out=k_grouped[u][:, i, :, :].rearrange("p (c j) m -> p c m j", j=4),
+                        in_=k_plain[u, i][:].rearrange("p m (c j) -> p c m j", j=4),
+                    )
+                else:
+                    nc.vector.tensor_tensor(
+                        out=k_grouped[u][:, i, :, :],
+                        in0=kt_banks[u][i][:].rearrange("p m s -> p s m"),
+                        in1=bias[:, w * E_TILES : (w + 1) * E_TILES].unsqueeze(1).to_broadcast([P, P, PACK]),
+                        op=ALU.add,
+                    )
 
         def quantise_k(u, tiles):
             if u not in k_operand:
@@ -381,6 +362,8 @@ def tile_slotmemoryphasor_pa_kernel(tc, x, Wk, bk, Wq, bq, slot_keys, scale, out
             score(1, both)
             quantise_x(3, both)
             project(3)
+            if by_scalar(3, 1):
+                scalar_bias(3, 1)
             find_shift(0, both)
             exponentials(0, both)
             quantise_w(1, 0, E)
@@ -398,8 +381,8 @@ def tile_slotmemoryphasor_pa_kernel(tc, x, Wk, bk, Wq, bq, slot_keys, scale, out
                     score(u, both)
                 if u + 1 <= last:
                     group_k(u + 1, both)
-                if u + 2 <= last and by_scalar(u + 2):
-                    scalar_bias(u + 2)
+                if u + 2 <= last and by_scalar(u + 2, 1):
+                    scalar_bias(u + 2, 1)
                 if u < last:
                     find_shift(u - 1, both)
                     exponentials(u - 1, both)

@@ -25,6 +25,9 @@ E_TILES = E // P
 SLOT_TILES = SLOTS // P
 ALIGN = 64
 
+VECTOR_NORMALISED = ((5, 0), (6, 0), (6, 1))
+SCALAR_NORMALISED = ((7, 0), (7, 1))
+
 SCALAR_UNITS = (3, 4, 5, 6, 7)
 
 FLOPS = PROJECTIONS * 2 * TOKENS * (D * E + E * SLOTS)
@@ -66,8 +69,8 @@ def tile_slotmemoryphasor_pa_kernel(tc, x, Wk, bk, Wq, bq, slot_keys, scale, out
                 in_=weights[w].rearrange("(h p r) e -> p h (r e)", h=2, r=2),
             )
 
-        load_x_tile(0, 0)
         load_w(0)
+        load_x_tile(0, 0)
         load_x_tile(0, 1)
         load_x(1)
         load_x(2)
@@ -175,6 +178,19 @@ def tile_slotmemoryphasor_pa_kernel(tc, x, Wk, bk, Wq, bq, slot_keys, scale, out
                 in_=slot_grouped[:].rearrange("p n t -> p (n t)"),
             )
 
+        def stay_warm(times):
+            idle = psum_t.tile([P, 4 * P], F32, tag="t")
+            for i in range(times):
+                nc.tensor.matmul_mx(
+                    out=idle[:],
+                    lhsT=w_codes[0][:, 0:P].bitcast(FP8X4),
+                    lhsT_scale=w_scales[0][:, 0:P],
+                    rhs=x_codes[:, 0 : 4 * P].bitcast(FP8X4),
+                    rhs_scale=x_scales[:, 0 : 4 * P],
+                    start=True,
+                    stop=True,
+                )
+
         kt_banks = {}
         k_plain = {}
         k_grouped = {}
@@ -268,16 +284,24 @@ def tile_slotmemoryphasor_pa_kernel(tc, x, Wk, bk, Wq, bq, slot_keys, scale, out
                 score_bank[u, i] = scores[:, j, :]
             score_bank[u] = scores
 
-        def find_shift(u, tiles):
+        def find_top(u, tiles):
             if u not in shifts:
                 top = work.tile([P, PAIR], F32)
                 shift = work.tile([P, PAIR], F32)
                 shifts[u] = (top, shift)
-            top, shift = shifts[u]
             cols = slice(tiles[0], tiles[-1] + 1)
             src = score_bank[u][:] if len(tiles) == PAIR else score_bank[u, tiles[0]]
-            nc.vector.tensor_reduce(out=top[:, cols], in_=src, axis=AXIS.X, op=ALU.max)
+            nc.vector.tensor_reduce(out=shifts[u][0][:, cols], in_=src, axis=AXIS.X, op=ALU.max)
+
+        def find_shift(u, tiles):
+            top, shift = shifts[u]
+            cols = slice(tiles[0], tiles[-1] + 1)
             nc.scalar.activation(out=shift[:, cols], in_=top[:, cols], func=ACT.Copy, scale=scale_neg_abs[:, 0:1])
+
+        def softmax_top(u, tiles):
+            find_top(u, tiles)
+            find_shift(u, tiles)
+            exponentials(u, tiles)
 
         def exponentials(u, tiles):
             if u not in exps:
@@ -303,12 +327,15 @@ def tile_slotmemoryphasor_pa_kernel(tc, x, Wk, bk, Wq, bq, slot_keys, scale, out
             cols = slice(tiles[0], tiles[-1] + 1)
             nc.vector.reciprocal(out=inverses[u][0][:, cols], in_=totals[u][:, cols])
 
-        def normalise_and_store(u, tiles):
-            w, c = units[u]
+        def normalise(u, tiles):
             inverse, prob = inverses[u]
             for i in tiles:
-                if u >= n_units - 2:
+                if (u, i) in VECTOR_NORMALISED:
                     nc.vector.tensor_scalar_mul(out=prob[:, i, :], in0=exps[u][:, i, :], scalar1=inverse[:, i : i + 1])
+                elif (u, i) in SCALAR_NORMALISED:
+                    nc.scalar.activation(
+                        out=prob[:, i, :], in_=exps[u][:, i, :], func=ACT.Copy, scale=inverse[:, i : i + 1]
+                    )
                 else:
                     nc.gpsimd.tensor_scalar(
                         out=prob[:, i, :],
@@ -318,6 +345,10 @@ def tile_slotmemoryphasor_pa_kernel(tc, x, Wk, bk, Wq, bq, slot_keys, scale, out
                         op0=ALU.mult,
                         op1=ALU.add,
                     )
+
+        def store(u, tiles):
+            w, c = units[u]
+            prob = inverses[u][1]
             cols = slice(tiles[0] * SLOTS, (tiles[-1] + 1) * SLOTS)
             nc.sync.dma_start(
                 out=out_pairs[w][c][:, cols], in_=prob[:, tiles[0] : tiles[-1] + 1, :].rearrange("p i n -> p (i n)")
@@ -328,32 +359,33 @@ def tile_slotmemoryphasor_pa_kernel(tc, x, Wk, bk, Wq, bq, slot_keys, scale, out
         half = E // 2
         with tc.manual_schedule():
             warm_up(4)
-            transpose_x(0, (0,))
-            warm_up(1)
             regroup_w(0, nc.vector.tensor_copy, 0, half)
             regroup_w(0, nc.scalar.copy, half + P, E)
+            transpose_x(0, (0,))
+            warm_up(1)
             transpose_x(0, (1,))
             warm_up(1)
-            quantise_x(0, (0,))
-            quantise_w(0, 0, half)
             regroup_w(0, nc.vector.tensor_copy, half, half + P)
-            quantise_x(0, (1,))
-            transpose_x(1, both)
-            warm_up(1)
+            quantise_w(0, 0, half)
+            quantise_x(0, (0,))
             quantise_w(0, half, E)
             prepare_bias()
-            quantise_x(1, both)
+            transpose_x(1, both)
+            quantise_x(0, (1,))
             project(0)
+            group_k(0, (0,))
+            quantise_x(1, both)
+            group_k(0, (1,))
             transpose_x(2, both)
             project(1)
             regroup_w(1, nc.scalar.copy, 0, half)
             transpose_slots()
-            group_k(0, both)
             quantise_x(2, both)
             quantise_k(0, both)
             project(2)
             transpose_x(3, both)
             regroup_w(1, nc.scalar.copy, half, E)
+            stay_warm(2)
             group_k(1, both)
             group_k(2, both)
             quantise_slots()
@@ -362,36 +394,54 @@ def tile_slotmemoryphasor_pa_kernel(tc, x, Wk, bk, Wq, bq, slot_keys, scale, out
             score(1, both)
             quantise_x(3, both)
             project(3)
-            if by_scalar(3, 1):
-                scalar_bias(3, 1)
-            find_shift(0, both)
-            exponentials(0, both)
+            scalar_bias(3, 1)
+            softmax_top(0, both)
             quantise_w(1, 0, E)
-            for u in range(2, n_units):
-                if u + 2 <= last:
-                    project(u + 2)
-                if u == last:
-                    find_shift(u - 1, both)
-                    exponentials(u - 1, both)
-                    for i in both:
-                        quantise_k(u, (i,))
-                        score(u, (i,))
-                else:
-                    quantise_k(u, both)
-                    score(u, both)
-                if u + 1 <= last:
-                    group_k(u + 1, both)
-                if u + 2 <= last and by_scalar(u + 2, 1):
-                    scalar_bias(u + 2, 1)
-                if u < last:
-                    find_shift(u - 1, both)
-                    exponentials(u - 1, both)
+            for u in range(2, last - 2):
+                project(u + 2)
+                quantise_k(u, both)
+                score(u, both)
+                group_k(u + 1, both)
+                scalar_bias(u + 2, 1)
+                softmax_top(u - 1, both)
                 invert_totals(u - 2, both)
-                normalise_and_store(u - 2, both)
+                normalise(u - 2, both)
+                store(u - 2, both)
+            project(last)
+            quantise_k(last - 2, both)
+            score(last - 2, both)
+            softmax_top(last - 3, both)
+            group_k(last - 1, both)
+            scalar_bias(last, 1)
+            invert_totals(last - 4, both)
+            normalise(last - 4, both)
+            store(last - 4, both)
+            softmax_top(last - 2, both)
+            quantise_k(last - 1, both)
+            score(last - 1, both)
+            stay_warm(4)
+            group_k(last, both)
+            invert_totals(last - 3, both)
+            normalise(last - 3, both)
+            store(last - 3, both)
+            quantise_k(last, (0,))
+            score(last, (0,))
+            softmax_top(last - 1, both)
+            quantise_k(last, (1,))
+            score(last, (1,))
+            invert_totals(last - 2, both)
             for i in both:
+                find_top(last, (i,))
                 find_shift(last, (i,))
+            normalise(last - 2, both)
+            store(last - 2, both)
+            invert_totals(last - 1, both)
+            for i in both:
+                normalise(last - 1, (i,))
+                store(last - 1, (i,))
+            for i in both:
                 exponentials(last, (i,))
-            for u in (last - 1, last):
-                for i in both:
-                    invert_totals(u, (i,))
-                    normalise_and_store(u, (i,))
+            for i in both:
+                invert_totals(last, (i,))
+                normalise(last, (i,))
+                store(last, (i,))

@@ -77,10 +77,12 @@ def tile_slotmemoryphasor_pa_kernel(tc, x, Wk, bk, Wq, bq, slot_keys, scale, out
         nc.sync.dma_start(out=slot_raw[:], in_=slot_keys.rearrange("(j p) e -> p j e", p=P))
         load_x(3)
         load_w(1)
-        nc.scalar.dma_start(out=scale_raw[:], in_=scale.partition_broadcast(P))
+        zeros = keep.tile([P, P], BF16)
         nc.vector.memset(bias_rows[:], 0.0)
+        nc.vector.memset(zeros[:], 0.0)
         nc.scalar.dma_start(out=bias_rows[0:E_TILES, :], in_=bk.rearrange("(m p) -> m p", p=P))
         nc.scalar.dma_start(out=bias_rows[E_TILES : 2 * E_TILES, :], in_=bq.rearrange("(m p) -> m p", p=P))
+        nc.scalar.dma_start(out=scale_raw[:], in_=scale.partition_broadcast(P))
 
         ident_f32 = keep.tile([P, P], F32)
         make_identity(nc, ident_f32[:])
@@ -88,19 +90,22 @@ def tile_slotmemoryphasor_pa_kernel(tc, x, Wk, bk, Wq, bq, slot_keys, scale, out
         make_identity(nc, ident_bf16[:])
 
         scale_sign = keep.tile([P, 1], F32)
-        nc.scalar.activation(out=scale_sign[:], in_=scale_raw[:], func=ACT.Sign)
         scale_abs = keep.tile([P, 1], F32)
-        nc.scalar.activation(out=scale_abs[:], in_=scale_raw[:], func=ACT.Abs)
         scale_neg_abs = keep.tile([P, 1], F32)
-        nc.scalar.mul(out=scale_neg_abs[:], in_=scale_abs[:], mul=-1.0)
 
-        zeros = keep.tile([P, 4 * P], BF16)
-        nc.vector.memset(zeros[:], 0.0)
+        def prepare_scale():
+            nc.scalar.activation(out=scale_sign[:], in_=scale_raw[:], func=ACT.Sign)
+            nc.scalar.activation(out=scale_abs[:], in_=scale_raw[:], func=ACT.Abs)
+            nc.scalar.mul(out=scale_neg_abs[:], in_=scale_abs[:], mul=-1.0)
+
+        first_exp = keep.tile([P, 1], F32)
+        nc.scalar.activation(out=first_exp[:], in_=zeros[:, 0:1], func=ACT.Exp)
+
 
         def warm_up(times):
             idle = psum_t.tile([P, 4 * P], F32, tag="t")
             for i in range(times):
-                nc.tensor.matmul(idle[:], zeros[:, 0:P], zeros[:], start=True, stop=True)
+                nc.tensor.matmul(idle[:], zeros[:], zeros[:, 0:1].to_broadcast([P, 4 * P]), start=True, stop=True)
 
         bias = keep.tile([P, PROJECTIONS * E_TILES], F32)
 
@@ -358,7 +363,7 @@ def tile_slotmemoryphasor_pa_kernel(tc, x, Wk, bk, Wq, bq, slot_keys, scale, out
         last = n_units - 1
         half = E // 2
         with tc.manual_schedule():
-            warm_up(4)
+            warm_up(5)
             regroup_w(0, nc.vector.tensor_copy, 0, half)
             regroup_w(0, nc.scalar.copy, half + P, E)
             transpose_x(0, (0,))
@@ -369,14 +374,15 @@ def tile_slotmemoryphasor_pa_kernel(tc, x, Wk, bk, Wq, bq, slot_keys, scale, out
             quantise_w(0, 0, half)
             quantise_x(0, (0,))
             quantise_w(0, half, E)
-            prepare_bias()
             transpose_x(1, both)
             quantise_x(0, (1,))
+            prepare_bias()
             project(0)
             group_k(0, (0,))
             quantise_x(1, both)
             group_k(0, (1,))
             transpose_x(2, both)
+            prepare_scale()
             project(1)
             regroup_w(1, nc.scalar.copy, 0, half)
             transpose_slots()
@@ -410,6 +416,7 @@ def tile_slotmemoryphasor_pa_kernel(tc, x, Wk, bk, Wq, bq, slot_keys, scale, out
             project(last)
             quantise_k(last - 2, both)
             score(last - 2, both)
+            stay_warm(3)
             softmax_top(last - 3, both)
             group_k(last - 1, both)
             scalar_bias(last, 1)
@@ -419,7 +426,7 @@ def tile_slotmemoryphasor_pa_kernel(tc, x, Wk, bk, Wq, bq, slot_keys, scale, out
             softmax_top(last - 2, both)
             quantise_k(last - 1, both)
             score(last - 1, both)
-            stay_warm(4)
+            stay_warm(1)
             group_k(last, both)
             invert_totals(last - 3, both)
             normalise(last - 3, both)

@@ -26,7 +26,7 @@ SLOT_TILES = SLOTS // P
 ALIGN = 64
 
 VECTOR_NORMALISED = ((5, 0), (6, 0), (6, 1))
-SCALAR_NORMALISED = ((7, 0), (7, 1))
+SCALAR_NORMALISED = ((3, 1), (4, 1), (7, 0), (7, 1))
 
 SCALAR_UNITS = (3, 4, 5, 6, 7)
 
@@ -112,7 +112,7 @@ def tile_slotmemoryphasor_pa_kernel(tc, x, Wk, bk, Wq, bq, slot_keys, scale, out
         def prepare_bias():
             bias_t = psum_t.tile([P, P], BF16, tag="t")
             nc.tensor.transpose(bias_t[:], bias_rows[:], ident_bf16[:])
-            nc.vector.tensor_copy(out=bias[:], in_=bias_t[:, 0 : PROJECTIONS * E_TILES])
+            nc.scalar.copy(out=bias[:], in_=bias_t[:, 0 : PROJECTIONS * E_TILES])
 
         x_grouped = [
             keep.tile([P, PAIR * P * PACK], BF16, name="x_grouped%d" % c, align_bytes=ALIGN) for c in range(N_PAIRS)
@@ -120,7 +120,9 @@ def tile_slotmemoryphasor_pa_kernel(tc, x, Wk, bk, Wq, bq, slot_keys, scale, out
         x_codes = keep.tile([P, TOKENS], U32, align_bytes=ALIGN)
         x_scales = keep.tile([P, TOKENS], U8, align_bytes=ALIGN)
 
-        def transpose_x(c, tiles):
+        x_turned = {}
+
+        def turn_x(c, tiles):
             words = x_raw[c][:].bitcast(F32)
             n = len(tiles)
             x_t = psum_t.tile([P, n, 2, P], F32, tag="t")
@@ -128,11 +130,20 @@ def tile_slotmemoryphasor_pa_kernel(tc, x, Wk, bk, Wq, bq, slot_keys, scale, out
                 for h in range(2):
                     first = (2 * i + h) * P
                     nc.tensor.transpose(x_t[:, j, h, :], words[:, first : first + P], ident_f32[:])
+            x_turned[c, tiles] = x_t
+
+        def drain_x(c, tiles):
+            n = len(tiles)
+            x_t = x_turned[c, tiles]
             cols = slice(tiles[0] * P * PACK, (tiles[-1] + 1) * P * PACK)
             nc.scalar.copy(
                 out=x_grouped[c][:, cols].bitcast(F32).rearrange("p (i s h) -> p i s h", i=n, h=2),
                 in_=x_t[:].rearrange("p i h s -> p i s h"),
             )
+
+        def transpose_x(c, tiles):
+            turn_x(c, tiles)
+            drain_x(c, tiles)
 
         def quantise_x(c, tiles):
             cols = slice((c * PAIR + tiles[0]) * P, (c * PAIR + tiles[-1] + 1) * P)
@@ -372,11 +383,12 @@ def tile_slotmemoryphasor_pa_kernel(tc, x, Wk, bk, Wq, bq, slot_keys, scale, out
             warm_up(1)
             regroup_w(0, nc.vector.tensor_copy, half, half + P)
             quantise_w(0, 0, half)
-            quantise_x(0, (0,))
             quantise_w(0, half, E)
-            transpose_x(1, both)
-            quantise_x(0, (1,))
+            quantise_x(0, (0,))
+            turn_x(1, both)
             prepare_bias()
+            drain_x(1, both)
+            quantise_x(0, (1,))
             project(0)
             group_k(0, (0,))
             quantise_x(1, both)
@@ -421,9 +433,11 @@ def tile_slotmemoryphasor_pa_kernel(tc, x, Wk, bk, Wq, bq, slot_keys, scale, out
             group_k(last - 1, both)
             scalar_bias(last, 1)
             invert_totals(last - 4, both)
+            find_top(last - 2, both)
+            find_shift(last - 2, both)
             normalise(last - 4, both)
             store(last - 4, both)
-            softmax_top(last - 2, both)
+            exponentials(last - 2, both)
             quantise_k(last - 1, both)
             score(last - 1, both)
             stay_warm(1)

@@ -63,13 +63,20 @@ def tile_slotmemoryphasor_pa_kernel(tc, x, Wk, bk, Wq, bq, slot_keys, scale, out
         def load_x_tile(c, i):
             nc.sync.dma_start(out=x_raw[c][:, i * D : (i + 1) * D], in_=x_pairs[c][:, i * D : (i + 1) * D])
 
+        def load_w_half(w, h, queue):
+            queue.dma_start(
+                out=w_raw[w][:, 2 * h : 2 * h + 2, :].rearrange("p r e -> p (r e)"),
+                in_=weights[w][h * 2 * P : (h + 1) * 2 * P, :].rearrange("(p r) e -> p (r e)", r=2),
+            )
+
         def load_w(w):
             nc.sync.dma_start(
                 out=w_raw[w][:].rearrange("p (h r) e -> p h (r e)", h=2),
                 in_=weights[w].rearrange("(h p r) e -> p h (r e)", h=2, r=2),
             )
 
-        load_w(0)
+        load_w_half(0, 0, nc.sync)
+        load_w_half(0, 1, nc.scalar)
         load_x_tile(0, 0)
         load_x_tile(0, 1)
         load_x(1)

from contextlib import ExitStack

import concourse.mybir as mybir
from concourse.masks import make_identity

F32 = mybir.dt.float32
BF16 = mybir.dt.bfloat16
U32 = mybir.dt.uint32
U8 = mybir.dt.uint8
FP8X4 = mybir.dt.float8_e4m3fn_x4
ACT = mybir.ActivationFunctionType
ALU = mybir.AluOpType
AXIS = mybir.AxisListType

P = 128
PACK = 4
TOKENS = 1024
D = P * PACK
E = P * PACK
SLOTS = 256
PROJECTIONS = 2
PAIR = 2
N_PAIRS = TOKENS // (PAIR * P)
E_TILES = E // P
SLOT_TILES = SLOTS // P
ALIGN = 64

VECTOR_NORMALISED = ((5, 0), (6, 0), (6, 1))
SCALAR_NORMALISED = ((3, 1), (4, 1), (7, 0), (7, 1))

SCALAR_UNITS = (3, 4, 5, 6, 7)

FLOPS = PROJECTIONS * 2 * TOKENS * (D * E + E * SLOTS)


def tile_slotmemoryphasor_pa_kernel(tc, x, Wk, bk, Wq, bq, slot_keys, scale, out_0, out_1):
    nc = tc.nc
    weights = (Wk, Wq)
    x_pairs = x.flatten_outer_dims().rearrange("(c p i) d -> c p (i d)", p=P, i=PAIR)
    out_pairs = (
        out_0.flatten_outer_dims().rearrange("(c p i) n -> c p (i n)", p=P, i=PAIR),
        out_1.flatten_outer_dims().rearrange("(c p i) n -> c p (i n)", p=P, i=PAIR),
    )
    units = [(w, c) for w in range(PROJECTIONS) for c in range(N_PAIRS)]
    n_units = len(units)

    with ExitStack() as ctx:
        keep = ctx.enter_context(tc.tile_pool(name="keep", bufs=1))
        work = ctx.enter_context(tc.tile_pool(name="work", bufs=n_units))
        psum_t = ctx.enter_context(tc.psum_pool(name="psum_t", bufs=4))
        psum_k = ctx.enter_context(tc.psum_pool(name="psum_k", bufs=2 * PAIR))


        x_raw = [keep.tile([P, PAIR * D], BF16, name="x_raw%d" % c) for c in range(N_PAIRS)]
        w_raw = [keep.tile([P, PACK, E], BF16, name="w_raw%d" % w) for w in range(PROJECTIONS)]
        slot_raw = keep.tile([P, SLOT_TILES, E], BF16)
        scale_raw = keep.tile([P, 1], BF16)
        bias_rows = keep.tile([P, P], BF16)

        def load_x(c):
            nc.sync.dma_start(out=x_raw[c][:], in_=x_pairs[c])

        def load_x_tile(c, i):
            nc.sync.dma_start(out=x_raw[c][:, i * D : (i + 1) * D], in_=x_pairs[c][:, i * D : (i + 1) * D])

        def load_w_half(w, h, queue):
            queue.dma_start(
                out=w_raw[w][:, 2 * h : 2 * h + 2, :].rearrange("p r e -> p (r e)"),
                in_=weights[w][h * 2 * P : (h + 1) * 2 * P, :].rearrange("(p r) e -> p (r e)", r=2),
            )

        def load_w(w):
            nc.sync.dma_start(
                out=w_raw[w][:].rearrange("p (h r) e -> p h (r e)", h=2),
                in_=weights[w].rearrange("(h p r) e -> p h (r e)", h=2, r=2),
            )

        load_w_half(0, 0, nc.sync)
        load_w_half(0, 1, nc.scalar)
        load_x_tile(0, 0)
        load_x_tile(0, 1)
        load_x(1)
        load_x(2)
        nc.sync.dma_start(out=slot_raw[:], in_=slot_keys.rearrange("(j p) e -> p j e", p=P))
        load_x(3)
        load_w(1)
        zeros = keep.tile([P, P], BF16)
        nc.vector.memset(bias_rows[:], 0.0)
        nc.vector.memset(zeros[:], 0.0)
        nc.scalar.dma_start(out=bias_rows[0:E_TILES, :], in_=bk.rearrange("(m p) -> m p", p=P))
        nc.scalar.dma_start(out=bias_rows[E_TILES : 2 * E_TILES, :], in_=bq.rearrange("(m p) -> m p", p=P))
        nc.scalar.dma_start(out=scale_raw[:], in_=scale.partition_broadcast(P))

        ident_f32 = keep.tile([P, P], F32)
        make_identity(nc, ident_f32[:])
        ident_bf16 = keep.tile([P, P], BF16)
        make_identity(nc, ident_bf16[:])

        scale_sign = keep.tile([P, 1], F32)
        scale_abs = keep.tile([P, 1], F32)
        scale_neg_abs = keep.tile([P, 1], F32)

        def prepare_scale():
            nc.scalar.activation(out=scale_sign[:], in_=scale_raw[:], func=ACT.Sign)
            nc.scalar.activation(out=scale_abs[:], in_=scale_raw[:], func=ACT.Abs)
            nc.scalar.mul(out=scale_neg_abs[:], in_=scale_abs[:], mul=-1.0)

        first_exp = keep.tile([P, 1], F32)
        nc.scalar.activation(out=first_exp[:], in_=zeros[:, 0:1], func=ACT.Exp)


        def warm_up(times):
            idle = psum_t.tile([P, 4 * P], F32, tag="t")
            for i in range(times):
                nc.tensor.matmul(idle[:], zeros[:], zeros[:, 0:1].to_broadcast([P, 4 * P]), start=True, stop=True)

        bias = keep.tile([P, PROJECTIONS * E_TILES], F32)

        def prepare_bias():
            bias_t = psum_t.tile([P, P], BF16, tag="t")
            nc.tensor.transpose(bias_t[:], bias_rows[:], ident_bf16[:])
            nc.scalar.copy(out=bias[:], in_=bias_t[:, 0 : PROJECTIONS * E_TILES])

        x_grouped = [
            keep.tile([P, PAIR * P * PACK], BF16, name="x_grouped%d" % c, align_bytes=ALIGN) for c in range(N_PAIRS)
        ]
        x_codes = keep.tile([P, TOKENS], U32, align_bytes=ALIGN)
        x_scales = keep.tile([P, TOKENS], U8, align_bytes=ALIGN)

        x_turned = {}

        def turn_x(c, tiles):
            words = x_raw[c][:].bitcast(F32)
            n = len(tiles)
            x_t = psum_t.tile([P, n, 2, P], F32, tag="t")
            for j, i in enumerate(tiles):
                for h in range(2):
                    first = (2 * i + h) * P
                    nc.tensor.transpose(x_t[:, j, h, :], words[:, first : first + P], ident_f32[:])
            x_turned[c, tiles] = x_t

        def drain_x(c, tiles):
            n = len(tiles)
            x_t = x_turned[c, tiles]
            cols = slice(tiles[0] * P * PACK, (tiles[-1] + 1) * P * PACK)
            nc.scalar.copy(
                out=x_grouped[c][:, cols].bitcast(F32).rearrange("p (i s h) -> p i s h", i=n, h=2),
                in_=x_t[:].rearrange("p i h s -> p i s h"),
            )

        def transpose_x(c, tiles):
            turn_x(c, tiles)
            drain_x(c, tiles)

        def quantise_x(c, tiles):
            cols = slice((c * PAIR + tiles[0]) * P, (c * PAIR + tiles[-1] + 1) * P)
            src = slice(tiles[0] * P * PACK, (tiles[-1] + 1) * P * PACK)
            nc.vector.quantize_mx(out=x_codes[:, cols].bitcast(FP8X4), scales=x_scales[:, cols], in_=x_grouped[c][:, src])

        w_grouped = [
            keep.tile([P, E, PACK], BF16, name="w_grouped%d" % w, align_bytes=ALIGN) for w in range(PROJECTIONS)
        ]
        w_codes = [keep.tile([P, E], U32, name="w_codes%d" % w, align_bytes=ALIGN) for w in range(PROJECTIONS)]
        w_scales = [keep.tile([P, E], U8, name="w_scales%d" % w, align_bytes=ALIGN) for w in range(PROJECTIONS)]

        def regroup_w(w, copy, first, last):
            copy(
                out=w_grouped[w][:, first:last, :].rearrange("p (c i) t -> p c t i", i=4),
                in_=w_raw[w][:, :, first:last].rearrange("p t (c i) -> p c t i", i=4),
            )

        def quantise_w(w, first, last):
            nc.vector.quantize_mx(
                out=w_codes[w][:, first:last].bitcast(FP8X4),
                scales=w_scales[w][:, first:last],
                in_=w_grouped[w][:, first:last, :].rearrange("p e t -> p (e t)"),
            )

        slot_grouped = keep.tile([P, SLOTS, PACK], BF16, align_bytes=ALIGN)
        slot_codes = keep.tile([P, SLOTS], U32, align_bytes=ALIGN)
        slot_scales = keep.tile([P, SLOTS], U8, align_bytes=ALIGN)

        def transpose_slots():
            slot_t = psum_t.tile([P, PACK, SLOTS], BF16, tag="t")
            for j in range(SLOT_TILES):
                for t in range(PACK):
                    nc.tensor.transpose(
                        slot_t[:, t, j * P : (j + 1) * P], slot_raw[:, j, t * P : (t + 1) * P], ident_bf16[:]
                    )
            nc.scalar.activation(
                out=slot_grouped[:],
                in_=slot_t[:].rearrange("p t n -> p n t"),
                func=ACT.Copy,
                scale=scale_sign[:, 0:1],
            )

        def quantise_slots():
            nc.vector.quantize_mx(
                out=slot_codes[:].bitcast(FP8X4),
                scales=slot_scales[:],
                in_=slot_grouped[:].rearrange("p n t -> p (n t)"),
            )

        def stay_warm(times):
            idle = psum_t.tile([P, 4 * P], F32, tag="t")
            for i in range(times):
                nc.tensor.matmul_mx(
                    out=idle[:],
                    lhsT=w_codes[0][:, 0:P].bitcast(FP8X4),
                    lhsT_scale=w_scales[0][:, 0:P],
                    rhs=x_codes[:, 0 : 4 * P].bitcast(FP8X4),
                    rhs_scale=x_scales[:, 0 : 4 * P],
                    start=True,
                    stop=True,
                )

        kt_banks = {}
        k_plain = {}
        k_grouped = {}
        k_operand = {}
        score_bank = {}
        shifts = {}
        exps = {}
        totals = {}
        inverses = {}

        def by_scalar(u, i):
            return i == 1 and u in SCALAR_UNITS

        def project(u):
            w, c = units[u]
            kt_banks[u] = []
            for i in range(PAIR):
                tokens = slice((c * PAIR + i) * P, (c * PAIR + i + 1) * P)
                kt = psum_k.tile([P, E_TILES, P], F32, tag="kt")
                for m in range(E_TILES):
                    e_cols = slice(m * P, (m + 1) * P)
                    nc.tensor.matmul_mx(
                        out=kt[:, m, :],
                        lhsT=w_codes[w][:, e_cols].bitcast(FP8X4),
                        lhsT_scale=w_scales[w][:, e_cols],
                        rhs=x_codes[:, tokens].bitcast(FP8X4),
                        rhs_scale=x_scales[:, tokens],
                        start=True,
                        stop=True,
                    )
                kt_banks[u].append(kt)

        def scalar_bias(u, i):
            w, c = units[u]
            plain = work.tile([P, E_TILES, P], BF16)
            for m in range(E_TILES):
                nc.scalar.activation(
                    out=plain[:, m, :],
                    in_=kt_banks[u][i][:, m, :],
                    func=ACT.Identity,
                    bias=bias[:, w * E_TILES + m : w * E_TILES + m + 1],
                )
            k_plain[u, i] = plain

        def group_k(u, tiles):
            w, c = units[u]
            if u not in k_grouped:
                grouped = work.tile([P, PAIR, P, PACK], BF16, align_bytes=ALIGN)
                k_grouped[u] = grouped
            for i in tiles:
                if by_scalar(u, i):
                    nc.vector.tensor_copy(
                        out=k_grouped[u][:, i, :, :].rearrange("p (c j) m -> p c m j", j=4),
                        in_=k_plain[u, i][:].rearrange("p m (c j) -> p c m j", j=4),
                    )
                else:
                    nc.vector.tensor_tensor(
                        out=k_grouped[u][:, i, :, :],
                        in0=kt_banks[u][i][:].rearrange("p m s -> p s m"),
                        in1=bias[:, w * E_TILES : (w + 1) * E_TILES].unsqueeze(1).to_broadcast([P, P, PACK]),
                        op=ALU.add,
                    )

        def quantise_k(u, tiles):
            if u not in k_operand:
                codes = work.tile([P, PAIR * P], U32, align_bytes=ALIGN)
                scales = work.tile([P, PAIR * P], U8, align_bytes=ALIGN)
                k_operand[u] = (codes, scales)
            codes, scales = k_operand[u]
            cols = slice(tiles[0] * P, (tiles[-1] + 1) * P)
            nc.vector.quantize_mx(
                out=codes[:, cols].bitcast(FP8X4),
                scales=scales[:, cols],
                in_=k_grouped[u][:, tiles[0] : tiles[-1] + 1, :, :].rearrange("p i s m -> p (i s m)"),
            )

        def score(u, tiles):
            codes, scales = k_operand[u]
            scores = psum_t.tile([P, len(tiles), SLOTS], F32, tag="t")
            for j, i in enumerate(tiles):
                tokens = slice(i * P, (i + 1) * P)
                nc.tensor.matmul_mx(
                    out=scores[:, j, :],
                    lhsT=codes[:, tokens].bitcast(FP8X4),
                    lhsT_scale=scales[:, tokens],
                    rhs=slot_codes[:].bitcast(FP8X4),
                    rhs_scale=slot_scales[:],
                    start=True,
                    stop=True,
                )
                score_bank[u, i] = scores[:, j, :]
            score_bank[u] = scores

        def find_top(u, tiles):
            if u not in shifts:
                top = work.tile([P, PAIR], F32)
                shift = work.tile([P, PAIR], F32)
                shifts[u] = (top, shift)
            cols = slice(tiles[0], tiles[-1] + 1)
            src = score_bank[u][:] if len(tiles) == PAIR else score_bank[u, tiles[0]]
            nc.vector.tensor_reduce(out=shifts[u][0][:, cols], in_=src, axis=AXIS.X, op=ALU.max)

        def find_shift(u, tiles):
            top, shift = shifts[u]
            cols = slice(tiles[0], tiles[-1] + 1)
            nc.scalar.activation(out=shift[:, cols], in_=top[:, cols], func=ACT.Copy, scale=scale_neg_abs[:, 0:1])

        def softmax_top(u, tiles):
            find_top(u, tiles)
            find_shift(u, tiles)
            exponentials(u, tiles)

        def exponentials(u, tiles):
            if u not in exps:
                e = work.tile([P, PAIR, SLOTS], F32)
                exps[u] = e
                total = work.tile([P, PAIR], F32)
                totals[u] = total
            for i in tiles:
                nc.scalar.activation(
                    out=exps[u][:, i, :],
                    in_=score_bank[u, i],
                    func=ACT.Exp,
                    bias=shifts[u][1][:, i : i + 1],
                    scale=scale_abs[:, 0:1],
                    accum_out=totals[u][:, i : i + 1],
                )

        def invert_totals(u, tiles):
            if u not in inverses:
                inverse = work.tile([P, PAIR], F32)
                prob = work.tile([P, PAIR, SLOTS], F32)
                inverses[u] = (inverse, prob)
            cols = slice(tiles[0], tiles[-1] + 1)
            nc.vector.reciprocal(out=inverses[u][0][:, cols], in_=totals[u][:, cols])

        def normalise(u, tiles):
            inverse, prob = inverses[u]
            for i in tiles:
                if (u, i) in VECTOR_NORMALISED:
                    nc.vector.tensor_scalar_mul(out=prob[:, i, :], in0=exps[u][:, i, :], scalar1=inverse[:, i : i + 1])
                elif (u, i) in SCALAR_NORMALISED:
                    nc.scalar.activation(
                        out=prob[:, i, :], in_=exps[u][:, i, :], func=ACT.Copy, scale=inverse[:, i : i + 1]
                    )
                else:
                    nc.gpsimd.tensor_scalar(
                        out=prob[:, i, :],
                        in0=exps[u][:, i, :],
                        scalar1=inverse[:, i : i + 1],
                        scalar2=0.0,
                        op0=ALU.mult,
                        op1=ALU.add,
                    )

        def store(u, tiles):
            w, c = units[u]
            prob = inverses[u][1]
            cols = slice(tiles[0] * SLOTS, (tiles[-1] + 1) * SLOTS)
            nc.sync.dma_start(
                out=out_pairs[w][c][:, cols], in_=prob[:, tiles[0] : tiles[-1] + 1, :].rearrange("p i n -> p (i n)")
            )

        both = (0, 1)
        last = n_units - 1
        half = E // 2
        with tc.manual_schedule():
            warm_up(5)
            regroup_w(0, nc.vector.tensor_copy, 0, half)
            regroup_w(0, nc.scalar.copy, half + P, E)
            transpose_x(0, (0,))
            warm_up(1)
            transpose_x(0, (1,))
            warm_up(1)
            regroup_w(0, nc.vector.tensor_copy, half, half + P)
            quantise_w(0, 0, half)
            quantise_w(0, half, E)
            quantise_x(0, (0,))
            turn_x(1, both)
            prepare_bias()
            drain_x(1, both)
            quantise_x(0, (1,))
            project(0)
            group_k(0, (0,))
            quantise_x(1, both)
            group_k(0, (1,))
            transpose_x(2, both)
            prepare_scale()
            project(1)
            regroup_w(1, nc.scalar.copy, 0, half)
            transpose_slots()
            quantise_x(2, both)
            quantise_k(0, both)
            project(2)
            transpose_x(3, both)
            regroup_w(1, nc.scalar.copy, half, E)
            stay_warm(2)
            group_k(1, both)
            group_k(2, both)
            quantise_slots()
            score(0, both)
            quantise_k(1, both)
            score(1, both)
            quantise_x(3, both)
            project(3)
            scalar_bias(3, 1)
            softmax_top(0, both)
            quantise_w(1, 0, E)
            for u in range(2, last - 2):
                project(u + 2)
                quantise_k(u, both)
                score(u, both)
                group_k(u + 1, both)
                scalar_bias(u + 2, 1)
                softmax_top(u - 1, both)
                invert_totals(u - 2, both)
                normalise(u - 2, both)
                store(u - 2, both)
            project(last)
            quantise_k(last - 2, both)
            score(last - 2, both)
            stay_warm(3)
            softmax_top(last - 3, both)
            group_k(last - 1, both)
            scalar_bias(last, 1)
            invert_totals(last - 4, both)
            find_top(last - 2, both)
            find_shift(last - 2, both)
            normalise(last - 4, both)
            store(last - 4, both)
            exponentials(last - 2, both)
            quantise_k(last - 1, both)
            score(last - 1, both)
            stay_warm(1)
            group_k(last, both)
            invert_totals(last - 3, both)
            normalise(last - 3, both)
            store(last - 3, both)
            quantise_k(last, (0,))
            score(last, (0,))
            softmax_top(last - 1, both)
            quantise_k(last, (1,))
            score(last, (1,))
            invert_totals(last - 2, both)
            for i in both:
                find_top(last, (i,))
                find_shift(last, (i,))
            normalise(last - 2, both)
            store(last - 2, both)
            invert_totals(last - 1, both)
            for i in both:
                normalise(last - 1, (i,))
                store(last - 1, (i,))
            for i in both:
                exponentials(last, (i,))
            for i in both:
                invert_totals(last, (i,))
                normalise(last, (i,))
                store(last, (i,))
